import numpy as np
import ml_dtypes


def mxq(x, axis, fmt="e4m3"):
    dtype, down = {"e4m3": (ml_dtypes.float8_e4m3fn, 7), "e5m2": (ml_dtypes.float8_e5m2, 14)}[fmt]
    v = np.moveaxis(np.asarray(x, np.float32).astype(ml_dtypes.bfloat16).astype(np.float64), axis, -1)
    blocks = v.reshape(v.shape[:-1] + (-1, 32))
    amax = np.abs(blocks).max(-1, keepdims=True)
    byte = np.maximum(np.where(amax > 0, np.frexp(amax)[1] - 1 + 127, 0) - down, 1)
    scale = np.exp2(byte - 127.0)
    codes = (blocks / scale).astype(np.float32).astype(dtype).astype(np.float64)
    return np.moveaxis((codes * scale).reshape(v.shape), -1, axis)


WIDE = False


def mx_kscale(k):
    if not WIDE:
        return np.ones(k)
    levels = np.array([10, -10, 5, -5, 0])
    a = np.random.permutation(np.resize(levels, k // 512 * 4)).reshape(k // 512, 4)
    idx = np.arange(k)
    return np.exp2(a[idx // 512, idx % 128 // 32])


BF16 = ml_dtypes.bfloat16


def bf(x):
    return np.asarray(x, np.float32).astype(BF16)


def f64(x):
    return np.asarray(x).astype(np.float64)


E2M1 = np.array([0.0, 0.5, 1.0, 1.5, 2.0, 3.0, 4.0, 6.0, -0.0, -0.5, -1.0, -1.5, -2.0, -3.0, -4.0, -6.0])


def pack_weight(w, fmt):
    k, n = w.shape
    w = f64(bf(w)).reshape(k // 32, 32, n)
    amax = np.abs(w).max(1)
    if fmt == "e4m3":
        byte = np.frexp(amax)[1] - 1 + 127 - 7
    else:
        mant, ex = np.frexp(amax / 6.0)
        byte = np.where(mant > 0.5, ex, ex - 1) + 127
    byte = np.clip(np.where(amax > 0, byte, 1), 1, 254)
    scaled = (w * np.exp2(127.0 - byte)[:, None, :]).reshape(k, n).astype(np.float32)
    by_word = np.ascontiguousarray(scaled.reshape(k // 512, 128, 4, n).transpose(0, 1, 3, 2))
    if fmt == "e4m3":
        words = by_word.astype(ml_dtypes.float8_e4m3fn).view(np.uint8)
    else:
        c = by_word.astype(ml_dtypes.float4_e2m1fn).view(np.uint8) & 0xF
        words = c[..., 0::2] | (c[..., 1::2] << 4)
    return np.ascontiguousarray(words), np.ascontiguousarray(byte.astype(np.uint8).reshape(k // 512, 16, n))


def unpack_weight(words, scales, fmt):
    g, p, n, _ = words.shape
    if fmt == "e4m3":
        vals = np.ascontiguousarray(words).view(ml_dtypes.float8_e4m3fn).astype(np.float64)
    else:
        nib = np.empty((g, p, n, 4), np.uint8)
        nib[..., 0::2] = words & 0xF
        nib[..., 1::2] = words >> 4
        vals = E2M1[nib]
    vals = vals * np.repeat(np.exp2(scales.astype(np.float64) - 127.0), 8, axis=1)[..., None]
    return vals.transpose(0, 1, 3, 2).reshape(g * 512, n)


B, CIN, COUT, E, G, NC = 8192, 512, 256, 4, 2, 2
OMEGA_0 = 30.0
FMT = "e4m3"


def setup_inputs():
    s = mx_kscale(CIN)
    wb = np.sqrt(6.0 / CIN) / OMEGA_0
    in_feats = bf(np.random.standard_normal((B, CIN)) * s)
    tile_gate = bf(np.random.standard_normal((B, E)) / np.sqrt(E))
    stack = np.swapaxes(np.random.uniform(-wb, wb, (E, COUT, CIN)) / s, 1, 2)
    words, scales = pack_weight(np.ascontiguousarray(stack).reshape(-1, COUT), FMT)
    return {"in_feats": in_feats,
            "tile_gate": tile_gate,
            "W_words": words,
            "W_scales": scales}


def reference(in_feats, tile_gate, W_words, W_scales):
    xq = mxq(f64(in_feats), 1, "e4m3")
    wq = unpack_weight(W_words, W_scales, FMT).reshape(E, CIN, COUT)
    g = f64(tile_gate)
    out = np.zeros((B, COUT))
    for t in range(E):
        out = out + g[:, t:t + 1] * (xq @ wq[t])
    return np.sin(OMEGA_0 * out)

@@ -1,0 +1,214 @@
+import math
+from contextlib import ExitStack
+
+import concourse.mybir as mybir
+from concourse.masks import make_identity
+
+F32 = mybir.dt.float32
+BF16 = mybir.dt.bfloat16
+I32 = mybir.dt.int32
+U32 = mybir.dt.uint32
+U8 = mybir.dt.uint8
+FP8X4 = mybir.dt.float8_e4m3fn_x4
+ALU = mybir.AluOpType
+ACT = mybir.ActivationFunctionType
+
+P = 128
+ROWS = 8192
+K = 512
+N_OUT = 256
+EXPERTS = 4
+OMEGA = 30.0
+
+TILES = ROWS // P
+PAIRS = TILES // 2
+K_WORDS = K // 2
+BANK = 512
+
+XT_BANKS = 2
+PROD_BANKS = 6
+LOADS_AHEAD = 8
+SINE_LAG = 2
+
+TURNS = OMEGA / (2.0 * math.pi)
+ROUND = 12582912.0
+
+FLOPS = 2 * ROWS * K * EXPERTS * N_OUT
+
+
+def tile_sinelayer_loe_pa_t_e_kernel(tc, in_feats, tile_gate, W_words, W_scales, out):
+    nc = tc.nc
+    x_rows = in_feats.rearrange("(p j) k -> p j k", j=TILES)
+    out_rows = out.rearrange("(p j) n -> p j n", j=TILES)
+
+    with ExitStack() as ctx:
+        keep = ctx.enter_context(tc.tile_pool(name="keep", bufs=1))
+        xin = ctx.enter_context(tc.tile_pool(name="xin", bufs=LOADS_AHEAD + 4))
+        work = ctx.enter_context(tc.tile_pool(name="work", bufs=4))
+        psum_xt = ctx.enter_context(tc.psum_pool(name="psum_xt", bufs=XT_BANKS))
+        psum_prod = ctx.enter_context(tc.psum_pool(name="psum_prod", bufs=PROD_BANKS))
+        ctx.enter_context(tc.manual_schedule())
+
+        x_of = {}
+        xt_of = {}
+        grouped_of = {}
+        codes_of = {}
+        prods_of = {}
+        turns_of = {}
+        frac_of = {}
+
+        def load(q):
+            x_of[q] = xin.tile([P, 2, K], BF16, name="x")
+            nc.sync.dma_start(out=x_of[q][:], in_=x_rows[:, 2 * q : 2 * q + 2, :])
+
+        gate_bf = keep.tile([P, TILES * EXPERTS], BF16)
+        nc.scalar.dma_start(out=gate_bf[:], in_=tile_gate.rearrange("(p j) t -> p (j t)", j=TILES))
+
+        w_scales = keep.tile([P, EXPERTS * N_OUT], U8, align_bytes=64)
+        nc.vector.memset(w_scales[:].bitcast(I32), 0)
+
+        zero = keep.tile([P, 1], F32)
+        nc.vector.memset(zero[:], 0.0)
+        warm = keep.tile([P, 1], F32)
+        nc.scalar.activation(out=warm[:], in_=zero[:], func=ACT.Sin)
+
+        ident = keep.tile([P, P], F32)
+        make_identity(nc, ident[:])
+
+        for q in range(XT_BANKS):
+            load(q)
+
+        for quad in range(4):
+            nc.sync.dma_start(
+                out=w_scales[32 * quad : 32 * quad + 4, :]
+                .bitcast(I32)
+                .rearrange("r (g n) -> r g n", g=EXPERTS),
+                in_=W_scales[:, 4 * quad : 4 * quad + 4, :].rearrange("g r n -> r g n").bitcast(I32),
+            )
+
+        w_words = keep.tile([P, EXPERTS * N_OUT], U32, align_bytes=64)
+        nc.sync.dma_start(
+            out=w_words[:].bitcast(I32).rearrange("p (g n) -> p g n", g=EXPERTS),
+            in_=W_words.rearrange("g p n t -> p g (n t)").bitcast(I32),
+        )
+
+        for q in range(XT_BANKS, LOADS_AHEAD):
+            load(q)
+
+        gate_turns = keep.tile([P, TILES * EXPERTS], F32)
+        nc.vector.tensor_scalar(
+            out=gate_turns[:], in0=gate_bf[:], scalar1=TURNS, scalar2=None, op0=ALU.mult
+        )
+
+        def transpose(q):
+            x = x_of.pop(q)
+            xt = psum_xt.tile([P, 2, 2, P], F32, name="xt")
+            for i in range(2):
+                x_words = x[:, i, :].bitcast(F32)
+                for u in range(2):
+                    nc.tensor.transpose(xt[:, i, u, :], x_words[:, u:K_WORDS:2], ident[:])
+            xt_of[q] = xt
+
+        def regroup(q):
+            xt = xt_of.pop(q)
+            grouped = work.tile([P, 2 * K], BF16, align_bytes=64, name="grouped")
+            nc.scalar.copy(
+                out=grouped[:].bitcast(F32).rearrange("p (i r u) -> p i r u", i=2, u=2),
+                in_=xt[:].rearrange("p i u r -> p i r u"),
+            )
+            grouped_of[q] = grouped
+
+        def quantise(q):
+            grouped = grouped_of.pop(q)
+            codes = work.tile([P, 2 * P], U32, align_bytes=64, name="codes")
+            x_scales = work.tile([P, 2 * P], U8, align_bytes=64, name="x_scales")
+            nc.vector.quantize_mx(out=codes[:].bitcast(FP8X4), scales=x_scales[:], in_=grouped[:])
+            codes_of[q] = (codes, x_scales)
+
+        def multiply(q):
+            codes, x_scales = codes_of.pop(q)
+            prods = {}
+            for i in range(2):
+                rows = slice(i * P, (i + 1) * P)
+                for h in range(EXPERTS // 2):
+                    cols = slice(h * BANK, (h + 1) * BANK)
+                    prod = psum_prod.tile([P, BANK], F32, name="prod")
+                    nc.tensor.matmul_mx(
+                        out=prod[:],
+                        lhsT=codes[:, rows].bitcast(FP8X4),
+                        lhsT_scale=x_scales[:, rows],
+                        rhs=w_words[:, cols].bitcast(FP8X4),
+                        rhs_scale=w_scales[:, cols],
+                        start=True,
+                        stop=True,
+                    )
+                    prods[(i, 2 * h)] = prod[:, 0:N_OUT]
+                    prods[(i, 2 * h + 1)] = prod[:, N_OUT : 2 * N_OUT]
+            prods_of[q] = prods
+
+        def gate(q, i, t):
+            col = (2 * q + i) * EXPERTS + t
+            return gate_turns[:, col : col + 1]
+
+        def first_term(q):
+            turns = work.tile([P, 2, N_OUT], F32, name="turns")
+            for i in range(2):
+                nc.scalar.activation(
+                    out=turns[:, i, :], in_=prods_of[q][(i, 0)], func=ACT.Copy, scale=gate(q, i, 0)
+                )
+            turns_of[q] = turns
+
+        def other_terms(q):
+            prods = prods_of.pop(q)
+            turns = turns_of[q]
+            for t in range(1, EXPERTS):
+                for i in range(2):
+                    nc.vector.scalar_tensor_tensor(
+                        out=turns[:, i, :],
+                        in0=prods[(i, t)],
+                        scalar=gate(q, i, t),
+                        in1=turns[:, i, :],
+                        op0=ALU.mult,
+                        op1=ALU.add,
+                    )
+
+        def reduce_range(q):
+            turns = turns_of.pop(q)
+            whole = work.tile([P, 2, N_OUT], F32, name="whole")
+            nc.vector.tensor_scalar(
+                out=whole[:], in0=turns[:], scalar1=ROUND, scalar2=ROUND, op0=ALU.add, op1=ALU.subtract
+            )
+            frac = work.tile([P, 2, N_OUT], F32, name="frac")
+            nc.gpsimd.tensor_tensor(out=frac[:], in0=turns[:], in1=whole[:], op=ALU.subtract)
+            frac_of[q] = frac
+
+        def sine_and_store(q):
+            frac = frac_of.pop(q)
+            result = work.tile([P, 2, N_OUT], F32, name="result")
+            nc.scalar.activation(out=result[:], in_=frac[:], func=ACT.Sin, scale=2.0 * math.pi)
+            nc.sync.dma_start(out=out_rows[:, 2 * q : 2 * q + 2, :], in_=result[:])
+
+        for q in range(XT_BANKS):
+            transpose(q)
+        for q in range(XT_BANKS):
+            regroup(q)
+            quantise(q)
+        for q in range(PAIRS + SINE_LAG):
+            if q + LOADS_AHEAD < PAIRS:
+                load(q + LOADS_AHEAD)
+            if q < PAIRS:
+                multiply(q)
+                first_term(q)
+            if q % XT_BANKS == 0:
+                for ahead in range(q + XT_BANKS, min(q + 2 * XT_BANKS, PAIRS)):
+                    transpose(ahead)
+            if q >= SINE_LAG:
+                sine_and_store(q - SINE_LAG)
+            if q + XT_BANKS < PAIRS:
+                regroup(q + XT_BANKS)
+            if q < PAIRS:
+                other_terms(q)
+            if q + XT_BANKS < PAIRS:
+                quantise(q + XT_BANKS)
+            if q < PAIRS:
+                reduce_range(q)

@@ -128,10 +128,10 @@ def tile_sinelayer_loe_pa_t_e_kernel(tc, in_feats, tile_gate, W_words, W_scales,
         def multiply(q):
             codes, x_scales = codes_of.pop(q)
             prods = {}
-            for i in range(2):
-                rows = slice(i * P, (i + 1) * P)
-                for h in range(EXPERTS // 2):
-                    cols = slice(h * BANK, (h + 1) * BANK)
+            for h in range(EXPERTS // 2):
+                cols = slice(h * BANK, (h + 1) * BANK)
+                for i in range(2):
+                    rows = slice(i * P, (i + 1) * P)
                     prod = psum_prod.tile([P, BANK], F32, name="prod")
                     nc.tensor.matmul_mx(
                         out=prod[:],

@@ -179,14 +179,27 @@ def tile_sinelayer_loe_pa_t_e_kernel(tc, in_feats, tile_gate, W_words, W_scales,
                 out=whole[:], in0=turns[:], scalar1=ROUND, scalar2=ROUND, op0=ALU.add, op1=ALU.subtract
             )
             frac = work.tile([P, 2, N_OUT], F32, name="frac")
-            nc.gpsimd.tensor_tensor(out=frac[:], in0=turns[:], in1=whole[:], op=ALU.subtract)
+            if q < PAIRS - 1:
+                nc.gpsimd.tensor_tensor(out=frac[:], in0=turns[:], in1=whole[:], op=ALU.subtract)
+            else:
+                for i in range(2):
+                    nc.vector.tensor_tensor(
+                        out=frac[:, i, :], in0=turns[:, i, :], in1=whole[:, i, :], op=ALU.subtract
+                    )
             frac_of[q] = frac
 
         def sine_and_store(q):
             frac = frac_of.pop(q)
             result = work.tile([P, 2, N_OUT], F32, name="result")
-            nc.scalar.activation(out=result[:], in_=frac[:], func=ACT.Sin, scale=2.0 * math.pi)
-            nc.sync.dma_start(out=out_rows[:, 2 * q : 2 * q + 2, :], in_=result[:])
+            if q < PAIRS - 1:
+                nc.scalar.activation(out=result[:], in_=frac[:], func=ACT.Sin, scale=2.0 * math.pi)
+                nc.sync.dma_start(out=out_rows[:, 2 * q : 2 * q + 2, :], in_=result[:])
+            else:
+                for i in range(2):
+                    nc.scalar.activation(
+                        out=result[:, i, :], in_=frac[:, i, :], func=ACT.Sin, scale=2.0 * math.pi
+                    )
+                    nc.sync.dma_start(out=out_rows[:, 2 * q + i, :], in_=result[:, i, :])
 
         for q in range(XT_BANKS):
             transpose(q)

@@ -112,17 +112,29 @@ def tile_sinelayer_loe_pa_t_e_kernel(tc, in_feats, tile_gate, W_words, W_scales,
         def regroup(q):
             xt = xt_of.pop(q)
             grouped = work.tile([P, 2 * K], BF16, align_bytes=64, name="grouped")
-            nc.scalar.copy(
-                out=grouped[:].bitcast(F32).rearrange("p (i r u) -> p i r u", i=2, u=2),
-                in_=xt[:].rearrange("p i u r -> p i r u"),
-            )
+            out_words = grouped[:].bitcast(F32).rearrange("p (i r u) -> p i r u", i=2, u=2)
+            in_words = xt[:].rearrange("p i u r -> p i r u")
+            if q == 0:
+                for i in range(2):
+                    nc.scalar.copy(out=out_words[:, i], in_=in_words[:, i])
+            else:
+                nc.scalar.copy(out=out_words, in_=in_words)
             grouped_of[q] = grouped
 
         def quantise(q):
             grouped = grouped_of.pop(q)
             codes = work.tile([P, 2 * P], U32, align_bytes=64, name="codes")
             x_scales = work.tile([P, 2 * P], U8, align_bytes=64, name="x_scales")
-            nc.vector.quantize_mx(out=codes[:].bitcast(FP8X4), scales=x_scales[:], in_=grouped[:])
+            if q == 0:
+                for i in range(2):
+                    rows = slice(i * P, (i + 1) * P)
+                    nc.vector.quantize_mx(
+                        out=codes[:, rows].bitcast(FP8X4),
+                        scales=x_scales[:, rows],
+                        in_=grouped[:, i * K : (i + 1) * K],
+                    )
+            else:
+                nc.vector.quantize_mx(out=codes[:].bitcast(FP8X4), scales=x_scales[:], in_=grouped[:])
             codes_of[q] = (codes, x_scales)
 
         def multiply(q):
@@ -172,12 +184,24 @@ def tile_sinelayer_loe_pa_t_e_kernel(tc, in_feats, tile_gate, W_words, W_scales,
                         op1=ALU.add,
                     )
 
+        def scalar_rounds(q):
+            return q % 2 == 1 and q < PAIRS - 1
+
         def reduce_range(q):
             turns = turns_of.pop(q)
             whole = work.tile([P, 2, N_OUT], F32, name="whole")
-            nc.vector.tensor_scalar(
-                out=whole[:], in0=turns[:], scalar1=ROUND, scalar2=ROUND, op0=ALU.add, op1=ALU.subtract
-            )
+            if scalar_rounds(q):
+                shifted = work.tile([P, N_OUT], F32, name="shifted")
+                nc.scalar.activation(out=shifted[:], in_=turns[:, 0, :], func=ACT.Copy, bias=ROUND)
+                nc.vector.tensor_scalar(
+                    out=whole[:, 1, :], in0=turns[:, 1, :], scalar1=ROUND, scalar2=ROUND,
+                    op0=ALU.add, op1=ALU.subtract,
+                )
+                nc.scalar.activation(out=whole[:, 0, :], in_=shifted[:], func=ACT.Copy, bias=-ROUND)
+            else:
+                nc.vector.tensor_scalar(
+                    out=whole[:], in0=turns[:], scalar1=ROUND, scalar2=ROUND, op0=ALU.add, op1=ALU.subtract
+                )
             frac = work.tile([P, 2, N_OUT], F32, name="frac")
             if q < PAIRS - 1:
                 nc.gpsimd.tensor_tensor(out=frac[:], in0=turns[:], in1=whole[:], op=ALU.subtract)
@@ -206,21 +230,25 @@ def tile_sinelayer_loe_pa_t_e_kernel(tc, in_feats, tile_gate, W_words, W_scales,
         for q in range(XT_BANKS):
             regroup(q)
             quantise(q)
+        multiply(0)
+        first_term(0)
+        for q in range(XT_BANKS, 2 * XT_BANKS):
+            transpose(q)
         for q in range(PAIRS + SINE_LAG):
             if q + LOADS_AHEAD < PAIRS:
                 load(q + LOADS_AHEAD)
-            if q < PAIRS:
-                multiply(q)
-                first_term(q)
-            if q % XT_BANKS == 0:
-                for ahead in range(q + XT_BANKS, min(q + 2 * XT_BANKS, PAIRS)):
-                    transpose(ahead)
             if q >= SINE_LAG:
                 sine_and_store(q - SINE_LAG)
             if q + XT_BANKS < PAIRS:
                 regroup(q + XT_BANKS)
             if q < PAIRS:
                 other_terms(q)
+            if q + 1 < PAIRS:
+                multiply(q + 1)
+                first_term(q + 1)
+            if q % XT_BANKS == 1:
+                for ahead in range(q + XT_BANKS + 1, min(q + 2 * XT_BANKS + 1, PAIRS)):
+                    transpose(ahead)
             if q + XT_BANKS < PAIRS:
                 quantise(q + XT_BANKS)
             if q < PAIRS:

@@ -28,7 +28,7 @@ BANK = 512
 XT_BANKS = 2
 PROD_BANKS = 6
 LOADS_AHEAD = 8
-SINE_LAG = 2
+SINE_LAG = 3
 
 TURNS = OMEGA / (2.0 * math.pi)
 ROUND = 12582912.0
@@ -44,7 +44,7 @@ def tile_sinelayer_loe_pa_t_e_kernel(tc, in_feats, tile_gate, W_words, W_scales,
     with ExitStack() as ctx:
         keep = ctx.enter_context(tc.tile_pool(name="keep", bufs=1))
         xin = ctx.enter_context(tc.tile_pool(name="xin", bufs=LOADS_AHEAD + 4))
-        work = ctx.enter_context(tc.tile_pool(name="work", bufs=4))
+        work = ctx.enter_context(tc.tile_pool(name="work", bufs=5))
         psum_xt = ctx.enter_context(tc.psum_pool(name="psum_xt", bufs=XT_BANKS))
         psum_prod = ctx.enter_context(tc.psum_pool(name="psum_prod", bufs=PROD_BANKS))
         ctx.enter_context(tc.manual_schedule())
@@ -56,6 +56,9 @@ def tile_sinelayer_loe_pa_t_e_kernel(tc, in_feats, tile_gate, W_words, W_scales,
         prods_of = {}
         turns_of = {}
         frac_of = {}
+        whole_of = {}
+        shifted_of = {}
+        result_of = {}
 
         def load(q):
             x_of[q] = xin.tile([P, 2, K], BF16, name="x")
@@ -184,47 +187,63 @@ def tile_sinelayer_loe_pa_t_e_kernel(tc, in_feats, tile_gate, W_words, W_scales,
                         op1=ALU.add,
                     )
 
-        def scalar_rounds(q):
-            return q % 2 == 1 and q < PAIRS - 1
+        def scalar_tiles(q):
+            if q == PAIRS - 1:
+                return 0
+            if q == PAIRS - 2:
+                return 2
+            return 1 if q % 4 != 0 else 0
 
-        def reduce_range(q):
-            turns = turns_of.pop(q)
+        def shift(q):
             whole = work.tile([P, 2, N_OUT], F32, name="whole")
-            if scalar_rounds(q):
-                shifted = work.tile([P, N_OUT], F32, name="shifted")
-                nc.scalar.activation(out=shifted[:], in_=turns[:, 0, :], func=ACT.Copy, bias=ROUND)
-                nc.vector.tensor_scalar(
-                    out=whole[:, 1, :], in0=turns[:, 1, :], scalar1=ROUND, scalar2=ROUND,
-                    op0=ALU.add, op1=ALU.subtract,
+            whole_of[q] = whole
+            n = scalar_tiles(q)
+            if n > 0:
+                shifted = work.tile([P, 2, N_OUT], F32, name="shifted")
+                nc.scalar.activation(
+                    out=shifted[:, 0:n, :], in_=turns_of[q][:, 0:n, :], func=ACT.Copy, bias=ROUND
                 )
-                nc.scalar.activation(out=whole[:, 0, :], in_=shifted[:], func=ACT.Copy, bias=-ROUND)
-            else:
-                nc.vector.tensor_scalar(
-                    out=whole[:], in0=turns[:], scalar1=ROUND, scalar2=ROUND, op0=ALU.add, op1=ALU.subtract
+                shifted_of[q] = shifted
+
+        def unshift(q):
+            n = scalar_tiles(q)
+            if n > 0:
+                nc.scalar.activation(
+                    out=whole_of[q][:, 0:n, :], in_=shifted_of.pop(q)[:, 0:n, :], func=ACT.Copy,
+                    bias=-ROUND,
                 )
-            frac = work.tile([P, 2, N_OUT], F32, name="frac")
-            if q < PAIRS - 1:
-                nc.gpsimd.tensor_tensor(out=frac[:], in0=turns[:], in1=whole[:], op=ALU.subtract)
-            else:
-                for i in range(2):
-                    nc.vector.tensor_tensor(
-                        out=frac[:, i, :], in0=turns[:, i, :], in1=whole[:, i, :], op=ALU.subtract
-                    )
-            frac_of[q] = frac
 
-        def sine_and_store(q):
-            frac = frac_of.pop(q)
-            result = work.tile([P, 2, N_OUT], F32, name="result")
-            if q < PAIRS - 1:
-                nc.scalar.activation(out=result[:], in_=frac[:], func=ACT.Sin, scale=2.0 * math.pi)
-                nc.sync.dma_start(out=out_rows[:, 2 * q : 2 * q + 2, :], in_=result[:])
-            else:
-                for i in range(2):
-                    nc.scalar.activation(
-                        out=result[:, i, :], in_=frac[:, i, :], func=ACT.Sin, scale=2.0 * math.pi
-                    )
-                    nc.sync.dma_start(out=out_rows[:, 2 * q + i, :], in_=result[:, i, :])
+        def round_rest(q):
+            n = scalar_tiles(q)
+            if n < 2:
+                nc.vector.tensor_scalar(
+                    out=whole_of[q][:, n:2, :], in0=turns_of[q][:, n:2, :], scalar1=ROUND,
+                    scalar2=ROUND, op0=ALU.add, op1=ALU.subtract,
+                )
 
+        def subtract(engine, q, tiles):
+            if q not in frac_of:
+                frac = work.tile([P, 2, N_OUT], F32, name="frac")
+                frac_of[q] = frac
+            engine.tensor_tensor(
+                out=frac_of[q][:, tiles, :], in0=turns_of[q][:, tiles, :],
+                in1=whole_of[q][:, tiles, :], op=ALU.subtract,
+            )
+
+        def sine_and_store(q, tiles):
+            if q not in result_of:
+                result = work.tile([P, 2, N_OUT], F32, name="result")
+                result_of[q] = result
+            nc.scalar.activation(
+                out=result_of[q][:, tiles, :], in_=frac_of[q][:, tiles, :], func=ACT.Sin,
+                scale=2.0 * math.pi,
+            )
+            nc.sync.dma_start(
+                out=out_rows[:, 2 * q + tiles.start : 2 * q + tiles.stop, :],
+                in_=result_of[q][:, tiles, :],
+            )
+
+        both = slice(0, 2)
         for q in range(XT_BANKS):
             transpose(q)
         for q in range(XT_BANKS):
@@ -234,15 +253,18 @@ def tile_sinelayer_loe_pa_t_e_kernel(tc, in_feats, tile_gate, W_words, W_scales,
         first_term(0)
         for q in range(XT_BANKS, 2 * XT_BANKS):
             transpose(q)
-        for q in range(PAIRS + SINE_LAG):
+        for q in range(PAIRS):
             if q + LOADS_AHEAD < PAIRS:
                 load(q + LOADS_AHEAD)
+            if q >= 1:
+                shift(q - 1)
             if q >= SINE_LAG:
-                sine_and_store(q - SINE_LAG)
+                sine_and_store(q - SINE_LAG, both)
+            if q >= 1:
+                unshift(q - 1)
             if q + XT_BANKS < PAIRS:
                 regroup(q + XT_BANKS)
-            if q < PAIRS:
-                other_terms(q)
+            other_terms(q)
             if q + 1 < PAIRS:
                 multiply(q + 1)
                 first_term(q + 1)
@@ -251,5 +273,14 @@ def tile_sinelayer_loe_pa_t_e_kernel(tc, in_feats, tile_gate, W_words, W_scales,
                     transpose(ahead)
             if q + XT_BANKS < PAIRS:
                 quantise(q + XT_BANKS)
-            if q < PAIRS:
-                reduce_range(q)
+            if 1 <= q < PAIRS - 1:
+                round_rest(q - 1)
+                subtract(nc.gpsimd, q - 1, both)
+        subtract(nc.vector, PAIRS - 2, both)
+        shift(PAIRS - 1)
+        round_rest(PAIRS - 1)
+        sine_and_store(PAIRS - 3, both)
+        sine_and_store(PAIRS - 2, both)
+        for i in range(2):
+            subtract(nc.vector, PAIRS - 1, slice(i, i + 1))
+            sine_and_store(PAIRS - 1, slice(i, i + 1))

@@ -192,7 +192,7 @@ def tile_sinelayer_loe_pa_t_e_kernel(tc, in_feats, tile_gate, W_words, W_scales,
                 return 0
             if q == PAIRS - 2:
                 return 2
-            return 1 if q % 4 != 0 else 0
+            return 1
 
         def shift(q):
             whole = work.tile([P, 2, N_OUT], F32, name="whole")

@@ -271,11 +271,11 @@ def tile_sinelayer_loe_pa_t_e_kernel(tc, in_feats, tile_gate, W_words, W_scales,
             if q % XT_BANKS == 1:
                 for ahead in range(q + XT_BANKS + 1, min(q + 2 * XT_BANKS + 1, PAIRS)):
                     transpose(ahead)
-            if q + XT_BANKS < PAIRS:
-                quantise(q + XT_BANKS)
             if 1 <= q < PAIRS - 1:
                 round_rest(q - 1)
                 subtract(nc.gpsimd, q - 1, both)
+            if q + XT_BANKS < PAIRS:
+                quantise(q + XT_BANKS)
         subtract(nc.vector, PAIRS - 2, both)
         shift(PAIRS - 1)
         round_rest(PAIRS - 1)

@@ -103,6 +103,12 @@ def tile_sinelayer_loe_pa_t_e_kernel(tc, in_feats, tile_gate, W_words, W_scales,
             out=gate_turns[:], in0=gate_bf[:], scalar1=TURNS, scalar2=None, op0=ALU.mult
         )
 
+        groups = [[0], [1], [2]] + [[g, g + 1] for g in range(3, PAIRS - 1, 2)] + [[PAIRS - 1]]
+        group_of = {}
+        for members in groups:
+            for place, member in enumerate(members):
+                group_of[member] = (members, place)
+
         def transpose(q):
             x = x_of.pop(q)
             xt = psum_xt.tile([P, 2, 2, P], F32, name="xt")
@@ -114,21 +120,29 @@ def tile_sinelayer_loe_pa_t_e_kernel(tc, in_feats, tile_gate, W_words, W_scales,
 
         def regroup(q):
             xt = xt_of.pop(q)
-            grouped = work.tile([P, 2 * K], BF16, align_bytes=64, name="grouped")
-            out_words = grouped[:].bitcast(F32).rearrange("p (i r u) -> p i r u", i=2, u=2)
+            members, place = group_of[q]
+            if place == 0:
+                grouped_new = work.tile([P, 4 * K], BF16, align_bytes=64, name="grouped")
+                grouped_of[members[0]] = grouped_new
+            grouped = grouped_of[members[0]]
+            out_words = (
+                grouped[:, place * 2 * K : (place + 1) * 2 * K]
+                .bitcast(F32)
+                .rearrange("p (i r u) -> p i r u", i=2, u=2)
+            )
             in_words = xt[:].rearrange("p i u r -> p i r u")
             if q == 0:
                 for i in range(2):
                     nc.scalar.copy(out=out_words[:, i], in_=in_words[:, i])
             else:
                 nc.scalar.copy(out=out_words, in_=in_words)
-            grouped_of[q] = grouped
 
-        def quantise(q):
-            grouped = grouped_of.pop(q)
-            codes = work.tile([P, 2 * P], U32, align_bytes=64, name="codes")
-            x_scales = work.tile([P, 2 * P], U8, align_bytes=64, name="x_scales")
-            if q == 0:
+        def quantise(first):
+            members, place = group_of[first]
+            grouped = grouped_of.pop(first)
+            codes = work.tile([P, 4 * P], U32, align_bytes=64, name="codes")
+            x_scales = work.tile([P, 4 * P], U8, align_bytes=64, name="x_scales")
+            if first == 0:
                 for i in range(2):
                     rows = slice(i * P, (i + 1) * P)
                     nc.vector.quantize_mx(
@@ -137,16 +151,21 @@ def tile_sinelayer_loe_pa_t_e_kernel(tc, in_feats, tile_gate, W_words, W_scales,
                         in_=grouped[:, i * K : (i + 1) * K],
                     )
             else:
-                nc.vector.quantize_mx(out=codes[:].bitcast(FP8X4), scales=x_scales[:], in_=grouped[:])
-            codes_of[q] = (codes, x_scales)
+                n = len(members) * 2 * P
+                nc.vector.quantize_mx(
+                    out=codes[:, 0:n].bitcast(FP8X4), scales=x_scales[:, 0:n], in_=grouped[:, 0 : 4 * n]
+                )
+            for member in members:
+                codes_of[member] = (codes, x_scales)
 
         def multiply(q):
             codes, x_scales = codes_of.pop(q)
+            base = group_of[q][1] * 2 * P
             prods = {}
             for h in range(EXPERTS // 2):
                 cols = slice(h * BANK, (h + 1) * BANK)
                 for i in range(2):
-                    rows = slice(i * P, (i + 1) * P)
+                    rows = slice(base + i * P, base + (i + 1) * P)
                     prod = psum_prod.tile([P, BANK], F32, name="prod")
                     nc.tensor.matmul_mx(
                         out=prod[:],
@@ -187,39 +206,43 @@ def tile_sinelayer_loe_pa_t_e_kernel(tc, in_feats, tile_gate, W_words, W_scales,
                         op1=ALU.add,
                     )
 
-        def scalar_tiles(q):
-            if q == PAIRS - 1:
-                return 0
-            if q == PAIRS - 2:
-                return 2
-            return 1
-
-        def shift(q):
+        def new_whole(q):
             whole = work.tile([P, 2, N_OUT], F32, name="whole")
             whole_of[q] = whole
-            n = scalar_tiles(q)
-            if n > 0:
-                shifted = work.tile([P, 2, N_OUT], F32, name="shifted")
-                nc.scalar.activation(
-                    out=shifted[:, 0:n, :], in_=turns_of[q][:, 0:n, :], func=ACT.Copy, bias=ROUND
-                )
-                shifted_of[q] = shifted
 
-        def unshift(q):
-            n = scalar_tiles(q)
-            if n > 0:
-                nc.scalar.activation(
-                    out=whole_of[q][:, 0:n, :], in_=shifted_of.pop(q)[:, 0:n, :], func=ACT.Copy,
-                    bias=-ROUND,
-                )
+        def shift(q):
+            shifted = work.tile([P, 2, N_OUT], F32, name="shifted")
+            nc.scalar.activation(out=shifted[:], in_=turns_of[q][:], func=ACT.Copy, bias=ROUND)
+            shifted_of[q] = shifted
 
-        def round_rest(q):
-            n = scalar_tiles(q)
-            if n < 2:
-                nc.vector.tensor_scalar(
-                    out=whole_of[q][:, n:2, :], in0=turns_of[q][:, n:2, :], scalar1=ROUND,
-                    scalar2=ROUND, op0=ALU.add, op1=ALU.subtract,
-                )
+        def unshift_scalar(q, tiles):
+            nc.scalar.activation(
+                out=whole_of[q][:, tiles, :], in_=shifted_of[q][:, tiles, :], func=ACT.Copy, bias=-ROUND
+            )
+
+        def unshift_gpsimd(q, tiles):
+            nc.gpsimd.tensor_scalar(
+                out=whole_of[q][:, tiles, :], in0=shifted_of[q][:, tiles, :], scalar1=1.0,
+                scalar2=-ROUND, op0=ALU.mult, op1=ALU.add,
+            )
+
+        def flat(tile):
+            return tile[:].rearrange("p i n -> p (i n)")
+
+        def round_vector(q, c0=0):
+            nc.vector.tensor_scalar(
+                out=flat(whole_of[q])[:, c0:], in0=flat(turns_of[q])[:, c0:], scalar1=ROUND,
+                scalar2=ROUND, op0=ALU.add, op1=ALU.subtract,
+            )
+
+        def round_scalar(q, c1):
+            part = work.tile([P, 2 * N_OUT], F32, name="part")
+            nc.scalar.activation(
+                out=part[:, 0:c1], in_=flat(turns_of[q])[:, 0:c1], func=ACT.Copy, bias=ROUND
+            )
+            nc.scalar.activation(
+                out=flat(whole_of[q])[:, 0:c1], in_=part[:, 0:c1], func=ACT.Copy, bias=-ROUND
+            )
 
         def subtract(engine, q, tiles):
             if q not in frac_of:
@@ -244,6 +267,7 @@ def tile_sinelayer_loe_pa_t_e_kernel(tc, in_feats, tile_gate, W_words, W_scales,
             )
 
         both = slice(0, 2)
+        S_COLS = 128
         for q in range(XT_BANKS):
             transpose(q)
         for q in range(XT_BANKS):
@@ -253,33 +277,46 @@ def tile_sinelayer_loe_pa_t_e_kernel(tc, in_feats, tile_gate, W_words, W_scales,
         first_term(0)
         for q in range(XT_BANKS, 2 * XT_BANKS):
             transpose(q)
+        regroup(2)
         for q in range(PAIRS):
+            odd = q % 2 == 1
             if q + LOADS_AHEAD < PAIRS:
                 load(q + LOADS_AHEAD)
-            if q >= 1:
+            if 0 < q < PAIRS - 3:
+                regroup(q + 3)
+            if odd and q >= 3:
+                sine_and_store(q - 3, both)
+            if q == PAIRS - 1:
+                new_whole(q - 1)
                 shift(q - 1)
-            if q >= SINE_LAG:
-                sine_and_store(q - SINE_LAG, both)
-            if q >= 1:
-                unshift(q - 1)
-            if q + XT_BANKS < PAIRS:
-                regroup(q + XT_BANKS)
+                unshift_scalar(q - 1, both)
+            elif odd:
+                new_whole(q - 1)
+                round_scalar(q - 1, S_COLS)
             other_terms(q)
             if q + 1 < PAIRS:
                 multiply(q + 1)
                 first_term(q + 1)
-            if q % XT_BANKS == 1:
-                for ahead in range(q + XT_BANKS + 1, min(q + 2 * XT_BANKS + 1, PAIRS)):
-                    transpose(ahead)
-            if 1 <= q < PAIRS - 1:
-                round_rest(q - 1)
+            if q == 0:
+                transpose(4)
+                regroup(3)
+            if q + 5 < PAIRS:
+                transpose(q + 5)
+            if odd and q >= 3:
+                sine_and_store(q - 2, both)
+            if q == 0:
+                quantise(2)
+            if odd and q < PAIRS - 1:
+                new_whole(q)
+                shift(q)
+                round_vector(q - 1, S_COLS)
                 subtract(nc.gpsimd, q - 1, both)
-            if q + XT_BANKS < PAIRS:
-                quantise(q + XT_BANKS)
+                quantise(q + 2)
+                unshift_gpsimd(q, both)
+                subtract(nc.gpsimd, q, both)
         subtract(nc.vector, PAIRS - 2, both)
-        shift(PAIRS - 1)
-        round_rest(PAIRS - 1)
-        sine_and_store(PAIRS - 3, both)
+        new_whole(PAIRS - 1)
+        round_vector(PAIRS - 1)
         sine_and_store(PAIRS - 2, both)
         for i in range(2):
             subtract(nc.vector, PAIRS - 1, slice(i, i + 1))

@@ -284,8 +284,6 @@ def tile_sinelayer_loe_pa_t_e_kernel(tc, in_feats, tile_gate, W_words, W_scales,
                 load(q + LOADS_AHEAD)
             if 0 < q < PAIRS - 3:
                 regroup(q + 3)
-            if odd and q >= 3:
-                sine_and_store(q - 3, both)
             if q == PAIRS - 1:
                 new_whole(q - 1)
                 shift(q - 1)
@@ -302,8 +300,8 @@ def tile_sinelayer_loe_pa_t_e_kernel(tc, in_feats, tile_gate, W_words, W_scales,
                 regroup(3)
             if q + 5 < PAIRS:
                 transpose(q + 5)
-            if odd and q >= 3:
-                sine_and_store(q - 2, both)
+            if q >= 3:
+                sine_and_store(q - 3, both)
             if q == 0:
                 quantise(2)
             if odd and q < PAIRS - 1:
@@ -317,6 +315,7 @@ def tile_sinelayer_loe_pa_t_e_kernel(tc, in_feats, tile_gate, W_words, W_scales,
         subtract(nc.vector, PAIRS - 2, both)
         new_whole(PAIRS - 1)
         round_vector(PAIRS - 1)
+        sine_and_store(PAIRS - 3, both)
         sine_and_store(PAIRS - 2, both)
         for i in range(2):
             subtract(nc.vector, PAIRS - 1, slice(i, i + 1))

@@ -103,7 +103,7 @@ def tile_sinelayer_loe_pa_t_e_kernel(tc, in_feats, tile_gate, W_words, W_scales,
             out=gate_turns[:], in0=gate_bf[:], scalar1=TURNS, scalar2=None, op0=ALU.mult
         )
 
-        groups = [[0], [1], [2]] + [[g, g + 1] for g in range(3, PAIRS - 1, 2)] + [[PAIRS - 1]]
+        groups = [[g] for g in range(5)] + [[g, g + 1] for g in range(5, PAIRS - 1, 2)] + [[PAIRS - 1]]
         group_of = {}
         for members in groups:
             for place, member in enumerate(members):
@@ -277,34 +277,42 @@ def tile_sinelayer_loe_pa_t_e_kernel(tc, in_feats, tile_gate, W_words, W_scales,
         first_term(0)
         for q in range(XT_BANKS, 2 * XT_BANKS):
             transpose(q)
-        regroup(2)
+        SINGLY = 3
         for q in range(PAIRS):
             odd = q % 2 == 1
+            if q < SINGLY:
+                copied = [q + 2]
+            elif q == SINGLY:
+                copied = [q + 2, q + 3]
+            else:
+                copied = [q + 3]
+            copied = [p for p in copied if p < PAIRS]
             if q + LOADS_AHEAD < PAIRS:
                 load(q + LOADS_AHEAD)
-            if 0 < q < PAIRS - 3:
-                regroup(q + 3)
+            for p in copied:
+                regroup(p)
             if q == PAIRS - 1:
                 new_whole(q - 1)
                 shift(q - 1)
                 unshift_scalar(q - 1, both)
-            elif odd:
+            elif 0 < q < SINGLY or odd:
                 new_whole(q - 1)
                 round_scalar(q - 1, S_COLS)
             other_terms(q)
             if q + 1 < PAIRS:
                 multiply(q + 1)
                 first_term(q + 1)
-            if q == 0:
-                transpose(4)
-                regroup(3)
-            if q + 5 < PAIRS:
-                transpose(q + 5)
+            for p in copied:
+                if p + 2 < PAIRS:
+                    transpose(p + 2)
             if q >= 3:
                 sine_and_store(q - 3, both)
-            if q == 0:
-                quantise(2)
-            if odd and q < PAIRS - 1:
+            if q < SINGLY:
+                if q > 0:
+                    round_vector(q - 1, S_COLS)
+                    subtract(nc.gpsimd, q - 1, both)
+                quantise(q + 2)
+            elif odd and q < PAIRS - 1:
                 new_whole(q)
                 shift(q)
                 round_vector(q - 1, S_COLS)

@@ -302,9 +302,11 @@ def tile_sinelayer_loe_pa_t_e_kernel(tc, in_feats, tile_gate, W_words, W_scales,
             if q + 1 < PAIRS:
                 multiply(q + 1)
                 first_term(q + 1)
-            for p in copied:
-                if p + 2 < PAIRS:
-                    transpose(p + 2)
+            if q < SINGLY:
+                transpose(q + 4)
+            elif odd:
+                for p in range(q + 4, min(q + 6, PAIRS)):
+                    transpose(p)
             if q >= 3:
                 sine_and_store(q - 3, both)
             if q < SINGLY:

@@ -267,7 +267,7 @@ def tile_sinelayer_loe_pa_t_e_kernel(tc, in_feats, tile_gate, W_words, W_scales,
             )
 
         both = slice(0, 2)
-        S_COLS = 128
+        S_COLS = 96
         for q in range(XT_BANKS):
             transpose(q)
         for q in range(XT_BANKS):

import math
from contextlib import ExitStack

import concourse.mybir as mybir
from concourse.masks import make_identity

F32 = mybir.dt.float32
BF16 = mybir.dt.bfloat16
I32 = mybir.dt.int32
U32 = mybir.dt.uint32
U8 = mybir.dt.uint8
FP8X4 = mybir.dt.float8_e4m3fn_x4
ALU = mybir.AluOpType
ACT = mybir.ActivationFunctionType

P = 128
ROWS = 8192
K = 512
N_OUT = 256
EXPERTS = 4
OMEGA = 30.0

TILES = ROWS // P
PAIRS = TILES // 2
K_WORDS = K // 2
BANK = 512

XT_BANKS = 2
PROD_BANKS = 6
LOADS_AHEAD = 8
SINE_LAG = 3

TURNS = OMEGA / (2.0 * math.pi)
ROUND = 12582912.0

FLOPS = 2 * ROWS * K * EXPERTS * N_OUT


def tile_sinelayer_loe_pa_t_e_kernel(tc, in_feats, tile_gate, W_words, W_scales, out):
    nc = tc.nc
    x_rows = in_feats.rearrange("(p j) k -> p j k", j=TILES)
    out_rows = out.rearrange("(p j) n -> p j n", j=TILES)

    with ExitStack() as ctx:
        keep = ctx.enter_context(tc.tile_pool(name="keep", bufs=1))
        xin = ctx.enter_context(tc.tile_pool(name="xin", bufs=LOADS_AHEAD + 4))
        work = ctx.enter_context(tc.tile_pool(name="work", bufs=5))
        psum_xt = ctx.enter_context(tc.psum_pool(name="psum_xt", bufs=XT_BANKS))
        psum_prod = ctx.enter_context(tc.psum_pool(name="psum_prod", bufs=PROD_BANKS))
        ctx.enter_context(tc.manual_schedule())

        x_of = {}
        xt_of = {}
        grouped_of = {}
        codes_of = {}
        prods_of = {}
        turns_of = {}
        frac_of = {}
        whole_of = {}
        shifted_of = {}
        result_of = {}

        def load(q):
            x_of[q] = xin.tile([P, 2, K], BF16, name="x")
            nc.sync.dma_start(out=x_of[q][:], in_=x_rows[:, 2 * q : 2 * q + 2, :])

        gate_bf = keep.tile([P, TILES * EXPERTS], BF16)
        nc.scalar.dma_start(out=gate_bf[:], in_=tile_gate.rearrange("(p j) t -> p (j t)", j=TILES))

        w_scales = keep.tile([P, EXPERTS * N_OUT], U8, align_bytes=64)
        nc.vector.memset(w_scales[:].bitcast(I32), 0)

        zero = keep.tile([P, 1], F32)
        nc.vector.memset(zero[:], 0.0)
        warm = keep.tile([P, 1], F32)
        nc.scalar.activation(out=warm[:], in_=zero[:], func=ACT.Sin)

        ident = keep.tile([P, P], F32)
        make_identity(nc, ident[:])

        for q in range(XT_BANKS):
            load(q)

        for quad in range(4):
            nc.sync.dma_start(
                out=w_scales[32 * quad : 32 * quad + 4, :]
                .bitcast(I32)
                .rearrange("r (g n) -> r g n", g=EXPERTS),
                in_=W_scales[:, 4 * quad : 4 * quad + 4, :].rearrange("g r n -> r g n").bitcast(I32),
            )

        w_words = keep.tile([P, EXPERTS * N_OUT], U32, align_bytes=64)
        nc.sync.dma_start(
            out=w_words[:].bitcast(I32).rearrange("p (g n) -> p g n", g=EXPERTS),
            in_=W_words.rearrange("g p n t -> p g (n t)").bitcast(I32),
        )

        for q in range(XT_BANKS, LOADS_AHEAD):
            load(q)

        gate_turns = keep.tile([P, TILES * EXPERTS], F32)
        nc.vector.tensor_scalar(
            out=gate_turns[:], in0=gate_bf[:], scalar1=TURNS, scalar2=None, op0=ALU.mult
        )

        groups = [[g] for g in range(5)] + [[g, g + 1] for g in range(5, PAIRS - 1, 2)] + [[PAIRS - 1]]
        group_of = {}
        for members in groups:
            for place, member in enumerate(members):
                group_of[member] = (members, place)

        def transpose(q):
            x = x_of.pop(q)
            xt = psum_xt.tile([P, 2, 2, P], F32, name="xt")
            for i in range(2):
                x_words = x[:, i, :].bitcast(F32)
                for u in range(2):
                    nc.tensor.transpose(xt[:, i, u, :], x_words[:, u:K_WORDS:2], ident[:])
            xt_of[q] = xt

        def regroup(q):
            xt = xt_of.pop(q)
            members, place = group_of[q]
            if place == 0:
                grouped_new = work.tile([P, 4 * K], BF16, align_bytes=64, name="grouped")
                grouped_of[members[0]] = grouped_new
            grouped = grouped_of[members[0]]
            out_words = (
                grouped[:, place * 2 * K : (place + 1) * 2 * K]
                .bitcast(F32)
                .rearrange("p (i r u) -> p i r u", i=2, u=2)
            )
            in_words = xt[:].rearrange("p i u r -> p i r u")
            if q == 0:
                for i in range(2):
                    nc.scalar.copy(out=out_words[:, i], in_=in_words[:, i])
            else:
                nc.scalar.copy(out=out_words, in_=in_words)

        def quantise(first):
            members, place = group_of[first]
            grouped = grouped_of.pop(first)
            codes = work.tile([P, 4 * P], U32, align_bytes=64, name="codes")
            x_scales = work.tile([P, 4 * P], U8, align_bytes=64, name="x_scales")
            if first == 0:
                for i in range(2):
                    rows = slice(i * P, (i + 1) * P)
                    nc.vector.quantize_mx(
                        out=codes[:, rows].bitcast(FP8X4),
                        scales=x_scales[:, rows],
                        in_=grouped[:, i * K : (i + 1) * K],
                    )
            else:
                n = len(members) * 2 * P
                nc.vector.quantize_mx(
                    out=codes[:, 0:n].bitcast(FP8X4), scales=x_scales[:, 0:n], in_=grouped[:, 0 : 4 * n]
                )
            for member in members:
                codes_of[member] = (codes, x_scales)

        def multiply(q):
            codes, x_scales = codes_of.pop(q)
            base = group_of[q][1] * 2 * P
            prods = {}
            for h in range(EXPERTS // 2):
                cols = slice(h * BANK, (h + 1) * BANK)
                for i in range(2):
                    rows = slice(base + i * P, base + (i + 1) * P)
                    prod = psum_prod.tile([P, BANK], F32, name="prod")
                    nc.tensor.matmul_mx(
                        out=prod[:],
                        lhsT=codes[:, rows].bitcast(FP8X4),
                        lhsT_scale=x_scales[:, rows],
                        rhs=w_words[:, cols].bitcast(FP8X4),
                        rhs_scale=w_scales[:, cols],
                        start=True,
                        stop=True,
                    )
                    prods[(i, 2 * h)] = prod[:, 0:N_OUT]
                    prods[(i, 2 * h + 1)] = prod[:, N_OUT : 2 * N_OUT]
            prods_of[q] = prods

        def gate(q, i, t):
            col = (2 * q + i) * EXPERTS + t
            return gate_turns[:, col : col + 1]

        def first_term(q):
            turns = work.tile([P, 2, N_OUT], F32, name="turns")
            for i in range(2):
                nc.scalar.activation(
                    out=turns[:, i, :], in_=prods_of[q][(i, 0)], func=ACT.Copy, scale=gate(q, i, 0)
                )
            turns_of[q] = turns

        def other_terms(q):
            prods = prods_of.pop(q)
            turns = turns_of[q]
            for t in range(1, EXPERTS):
                for i in range(2):
                    nc.vector.scalar_tensor_tensor(
                        out=turns[:, i, :],
                        in0=prods[(i, t)],
                        scalar=gate(q, i, t),
                        in1=turns[:, i, :],
                        op0=ALU.mult,
                        op1=ALU.add,
                    )

        def new_whole(q):
            whole = work.tile([P, 2, N_OUT], F32, name="whole")
            whole_of[q] = whole

        def shift(q):
            shifted = work.tile([P, 2, N_OUT], F32, name="shifted")
            nc.scalar.activation(out=shifted[:], in_=turns_of[q][:], func=ACT.Copy, bias=ROUND)
            shifted_of[q] = shifted

        def unshift_scalar(q, tiles):
            nc.scalar.activation(
                out=whole_of[q][:, tiles, :], in_=shifted_of[q][:, tiles, :], func=ACT.Copy, bias=-ROUND
            )

        def unshift_gpsimd(q, tiles):
            nc.gpsimd.tensor_scalar(
                out=whole_of[q][:, tiles, :], in0=shifted_of[q][:, tiles, :], scalar1=1.0,
                scalar2=-ROUND, op0=ALU.mult, op1=ALU.add,
            )

        def flat(tile):
            return tile[:].rearrange("p i n -> p (i n)")

        def round_vector(q, c0=0):
            nc.vector.tensor_scalar(
                out=flat(whole_of[q])[:, c0:], in0=flat(turns_of[q])[:, c0:], scalar1=ROUND,
                scalar2=ROUND, op0=ALU.add, op1=ALU.subtract,
            )

        def round_scalar(q, c1):
            part = work.tile([P, 2 * N_OUT], F32, name="part")
            nc.scalar.activation(
                out=part[:, 0:c1], in_=flat(turns_of[q])[:, 0:c1], func=ACT.Copy, bias=ROUND
            )
            nc.scalar.activation(
                out=flat(whole_of[q])[:, 0:c1], in_=part[:, 0:c1], func=ACT.Copy, bias=-ROUND
            )

        def subtract(engine, q, tiles):
            if q not in frac_of:
                frac = work.tile([P, 2, N_OUT], F32, name="frac")
                frac_of[q] = frac
            engine.tensor_tensor(
                out=frac_of[q][:, tiles, :], in0=turns_of[q][:, tiles, :],
                in1=whole_of[q][:, tiles, :], op=ALU.subtract,
            )

        def sine_and_store(q, tiles):
            if q not in result_of:
                result = work.tile([P, 2, N_OUT], F32, name="result")
                result_of[q] = result
            nc.scalar.activation(
                out=result_of[q][:, tiles, :], in_=frac_of[q][:, tiles, :], func=ACT.Sin,
                scale=2.0 * math.pi,
            )
            nc.sync.dma_start(
                out=out_rows[:, 2 * q + tiles.start : 2 * q + tiles.stop, :],
                in_=result_of[q][:, tiles, :],
            )

        both = slice(0, 2)
        S_COLS = 96
        for q in range(XT_BANKS):
            transpose(q)
        for q in range(XT_BANKS):
            regroup(q)
            quantise(q)
        multiply(0)
        first_term(0)
        for q in range(XT_BANKS, 2 * XT_BANKS):
            transpose(q)
        SINGLY = 3
        for q in range(PAIRS):
            odd = q % 2 == 1
            if q < SINGLY:
                copied = [q + 2]
            elif q == SINGLY:
                copied = [q + 2, q + 3]
            else:
                copied = [q + 3]
            copied = [p for p in copied if p < PAIRS]
            if q + LOADS_AHEAD < PAIRS:
                load(q + LOADS_AHEAD)
            for p in copied:
                regroup(p)
            if q == PAIRS - 1:
                new_whole(q - 1)
                shift(q - 1)
                unshift_scalar(q - 1, both)
            elif 0 < q < SINGLY or odd:
                new_whole(q - 1)
                round_scalar(q - 1, S_COLS)
            other_terms(q)
            if q + 1 < PAIRS:
                multiply(q + 1)
                first_term(q + 1)
            if q < SINGLY:
                transpose(q + 4)
            elif odd:
                for p in range(q + 4, min(q + 6, PAIRS)):
                    transpose(p)
            if q >= 3:
                sine_and_store(q - 3, both)
            if q < SINGLY:
                if q > 0:
                    round_vector(q - 1, S_COLS)
                    subtract(nc.gpsimd, q - 1, both)
                quantise(q + 2)
            elif odd and q < PAIRS - 1:
                new_whole(q)
                shift(q)
                round_vector(q - 1, S_COLS)
                subtract(nc.gpsimd, q - 1, both)
                quantise(q + 2)
                unshift_gpsimd(q, both)
                subtract(nc.gpsimd, q, both)
        subtract(nc.vector, PAIRS - 2, both)
        new_whole(PAIRS - 1)
        round_vector(PAIRS - 1)
        sine_and_store(PAIRS - 3, both)
        sine_and_store(PAIRS - 2, both)
        for i in range(2):
            subtract(nc.vector, PAIRS - 1, slice(i, i + 1))
            sine_and_store(PAIRS - 1, slice(i, i + 1))
